import numpy as np
import ml_dtypes


def mxq(x, axis, fmt="e4m3"):
    dtype, down = {"e4m3": (ml_dtypes.float8_e4m3fn, 7), "e5m2": (ml_dtypes.float8_e5m2, 14)}[fmt]
    v = np.moveaxis(np.asarray(x, np.float32).astype(ml_dtypes.bfloat16).astype(np.float64), axis, -1)
    blocks = v.reshape(v.shape[:-1] + (-1, 32))
    amax = np.abs(blocks).max(-1, keepdims=True)
    byte = np.maximum(np.where(amax > 0, np.frexp(amax)[1] - 1 + 127, 0) - down, 1)
    scale = np.exp2(byte - 127.0)
    codes = (blocks / scale).astype(np.float32).astype(dtype).astype(np.float64)
    return np.moveaxis((codes * scale).reshape(v.shape), -1, axis)


WIDE = False


def mx_kscale(k):
    if not WIDE:
        return np.ones(k)
    levels = np.array([10, -10, 5, -5, 0])
    if k % 512:
        return np.exp2(np.random.permutation(np.resize(levels, k // 32))).repeat(32)
    a = np.empty((k // 512, 16))
    for p in range(k // 512):
        a[p, :8] = np.random.permutation(np.resize(levels, 8))
        for g in range(8):
            far = levels[np.abs(levels - a[p, g]) >= 10]
            a[p, g + 8] = far[np.random.randint(len(far))]
    return np.exp2(a.ravel()).repeat(32)


BF16 = ml_dtypes.bfloat16


def bf(x):
    return np.asarray(x, np.float32).astype(BF16)


def f64(x):
    return np.asarray(x).astype(np.float64)


N, M, D, R = 2048, 2048, 512, 4


def softplus(x):
    return np.logaddexp(x, 0.0)


def setup_inputs():
    s = mx_kscale(N)[:, None]
    u = mx_kscale(M)
    basis = np.random.standard_normal((R, D)) / np.sqrt(D)
    X0 = bf(0.5 * np.random.standard_normal((N, R)) @ basis + 0.5 * np.random.standard_normal((N, D)) / np.sqrt(D))
    X20 = bf(0.5 * np.random.standard_normal((M, R)) @ basis + 0.5 * np.random.standard_normal((M, D)) / np.sqrt(D))
    raw1 = np.log(np.expm1(1.0))
    lengthscale = bf(raw1 + 0.3 * np.random.standard_normal((1, D)))
    variance = bf(1.5 + 0.3 * np.random.standard_normal(1))
    g = bf(16.0 * np.random.standard_normal((N, M)) * np.exp2(np.random.randint(-6, 1, (N, 1))) / s * u[None, :])
    l = softplus(f64(lengthscale))
    Xl = f64(X0) / l
    X2l = f64(X20) / l
    d2 = np.maximum(np.sum(Xl * Xl, axis=1)[:, None] + np.sum(X2l * X2l, axis=1)[None, :] - 2.0 * (Xl @ X2l.T), 0.0)
    return {"X": bf(f64(X0) * s), "X2": bf(f64(X20) / u[:, None]),
            "lengthscale": lengthscale, "variance": variance,
            "d2": np.asarray(d2, np.float32), "grad_out": g}


def reference(X, X2, lengthscale, variance, d2, grad_out):
    l = softplus(f64(lengthscale))
    v = softplus(f64(variance))
    d = f64(d2)
    W = f64(grad_out) * (v[0] * np.exp(-0.5 * d)) * (d > 0.0)
    r = np.sum(W, axis=1)[:, None]
    c = np.sum(W, axis=0)[:, None]
    Wb = W
    P = mxq(Wb, 1, "e5m2") @ mxq(f64(X2), 0, "e4m3")
    Q = mxq(Wb, 0, "e5m2").T @ mxq(f64(X), 0, "e4m3")
    dX = (P - f64(X) * r) / (l * l)
    dX2 = (Q - f64(X2) * c) / (l * l)
    return dX, dX2

@@ -1,0 +1,313 @@
+from contextlib import ExitStack
+
+import concourse.mybir as mybir
+from concourse.masks import make_identity
+
+FLOPS = 2 * 2 * 2048 * 2048 * 512
+
+F32 = mybir.dt.float32
+BF16 = mybir.dt.bfloat16
+U32 = mybir.dt.uint32
+U8 = mybir.dt.uint8
+E4 = mybir.dt.float8_e4m3fn_x4
+E5 = mybir.dt.float8_e5m2_x4
+ALU = mybir.AluOpType
+ACT = mybir.ActivationFunctionType
+AX = mybir.AxisListType
+
+P = 128
+G = 4
+T = 4
+KP = 512
+D = 512
+
+
+def block_order():
+    seq = []
+    for d in range(G):
+        for gj in range(d, G):
+            seq.append((d, gj))
+        for gi in range(d + 1, G):
+            seq.append((gi, d))
+    return seq
+
+
+def tile_rbf_t_v_kernel(tc, X, X2, lengthscale, variance, d2, grad_out, out_0, out_1):
+    nc = tc.nc
+    seq = block_order()
+    nb = len(seq)
+
+    d2v = d2.rearrange("(g p t) j -> p g t j", p=P, t=T)
+    gv = grad_out.rearrange("(g p t) j -> p g t j", p=P, t=T)
+    xv = X.rearrange("(g p t) k -> p g t k", p=P, t=T)
+    x2v = X2.rearrange("(g p t) k -> p g t k", p=P, t=T)
+    o0v = out_0.rearrange("(g p t) k -> p g t k", p=P, t=T)
+    o1v = out_1.rearrange("(g p t) k -> p g t k", p=P, t=T)
+
+    with ExitStack() as ctx:
+        ctx.enter_context(tc.manual_schedule())
+        const = ctx.enter_context(tc.tile_pool(name="const", bufs=1))
+        stream = ctx.enter_context(tc.tile_pool(name="stream", bufs=2))
+        codes = ctx.enter_context(tc.tile_pool(name="codes", bufs=1))
+        psum = ctx.enter_context(tc.psum_pool(name="psum", bufs=1))
+
+        prow = const.tile([P, 544], BF16, name="prow")
+        ones_bf = const.tile([P, P], BF16, name="ones_bf")
+        ones_f = const.tile([P, 8], F32, name="ones_f")
+        ident = const.tile([P, P], F32, name="ident")
+        nc.gpsimd.memset(prow[:], 0.0)
+        nc.gpsimd.memset(ones_bf[:], 1.0)
+        nc.gpsimd.memset(ones_f[:], 1.0)
+        make_identity(nc, ident[:])
+        nc.sync.dma_start(out=prow[0:1, 0:D], in_=lengthscale)
+        nc.sync.dma_start(out=prow[0:1, D:D + 1], in_=variance.rearrange("(o k) -> o k", o=1))
+
+        xn = const.tile([P, G, T, D], BF16, name="xn")
+        x2n = const.tile([P, G, T, D], BF16, name="x2n")
+        xc = const.tile([P, G, D], U32, name="xc", align_bytes=64)
+        xs = const.tile([P, G, D], U8, name="xs", align_bytes=64)
+        x2c = const.tile([P, G, D], U32, name="x2c", align_bytes=64)
+        x2s = const.tile([P, G, D], U8, name="x2s", align_bytes=64)
+        rpart = const.tile([P, G * T * G], F32, name="rpart")
+        rs = const.tile([P, G * T], F32, name="rs")
+        cs = const.tile([P, G * T], F32, name="cs")
+        cpart = psum.tile([P, G * T * G * T], F32, name="cpart", tag="cpart")
+
+        dtiles = {}
+        gtiles = {}
+
+        def load(n):
+            gi, gj = seq[n]
+            dt_ = stream.tile([P, T, KP], F32, name="dt_", tag="dt", bufs=3)
+            gt_ = stream.tile([P, T, KP], BF16, name="gt_", tag="gt", bufs=3)
+            nc.sync.dma_start(out=dt_[:], in_=d2v[:, gi, :, gj * KP:(gj + 1) * KP])
+            nc.sync.dma_start(out=gt_[:], in_=gv[:, gi, :, gj * KP:(gj + 1) * KP])
+            dtiles[n] = dt_
+            gtiles[n] = gt_
+
+        def load_x(which, g):
+            if which == 2:
+                nc.sync.dma_start(out=x2n[:, g], in_=x2v[:, g])
+            else:
+                nc.sync.dma_start(out=xn[:, g], in_=xv[:, g])
+
+        load(0)
+        load_x(2, 0)
+        load(1)
+        load_x(2, 1)
+
+        pb1 = psum.tile([P, D], F32, name="pb1", tag="mx", bufs=3)
+        pb2 = psum.tile([P, D], F32, name="pb2", tag="mx", bufs=3)
+        nc.tensor.matmul(out=pb1[:], lhsT=ones_bf[:], rhs=prow[:, 0:D], start=True, stop=True)
+        nc.tensor.matmul(out=pb2[:, 0:32], lhsT=ones_bf[:], rhs=prow[:, D:D + 32], start=True, stop=True)
+        x32 = const.tile([P, 544], F32, name="x32")
+        na = const.tile([P, 544], F32, name="na")
+        sp = const.tile([P, 544], F32, name="sp")
+        nil2 = const.tile([P, D], F32, name="nil2")
+        vcol = const.tile([P, 8], F32, name="vcol")
+        nc.vector.tensor_copy(out=x32[:, 0:D], in_=pb1[:])
+        nc.vector.tensor_copy(out=x32[:, D:D + 32], in_=pb2[:, 0:32])
+        nc.vector.scalar_tensor_tensor(out=na[:], in0=x32[:], scalar=-1.0, in1=x32[:], op0=ALU.mult, op1=ALU.min)
+        nc.scalar.activation(out=na[:], in_=na[:], func=ACT.Exp)
+        nc.scalar.activation(out=na[:], in_=na[:], func=ACT.Ln, bias=1.0)
+        nc.vector.scalar_tensor_tensor(out=sp[:], in0=x32[:], scalar=0.0, in1=na[:], op0=ALU.max, op1=ALU.add)
+        nc.vector.tensor_copy(out=vcol[:, 0:1], in_=sp[:, D:D + 1])
+        nc.vector.tensor_tensor(out=x32[:, 0:D], in0=sp[:, 0:D], in1=sp[:, 0:D], op=ALU.mult)
+        nc.vector.reciprocal(out=na[:, 0:D], in_=x32[:, 0:D])
+        nc.vector.tensor_scalar(out=nil2[:], in0=na[:, 0:D], scalar1=-1.0, scalar2=None, op0=ALU.mult)
+
+        etiles = {}
+        gmtiles = {}
+        wtiles = {}
+        trtiles = {}
+        abtiles = {}
+        bbtiles = {}
+        acodes = {}
+        bcodes = {}
+        free_a = list(range(16))
+        free_b = list(range(16))
+        slot_a = {}
+        slot_b = {}
+
+        def s_exp(n):
+            e = stream.tile([P, T, KP], F32, name="e", tag="e", bufs=2)
+            nc.scalar.activation(
+                out=e[:].rearrange("p t (u q) -> p t u q", u=T),
+                in_=dtiles[n][:].rearrange("p t (q u) -> p t u q", u=T),
+                func=ACT.Exp, scale=-0.5)
+            etiles[n] = e
+
+        def v_mask(n):
+            gm = stream.tile([P, T, KP], BF16, name="gm", tag="gm", bufs=2)
+            nc.vector.scalar_tensor_tensor(
+                out=gm[:].rearrange("p t j -> p (t j)"),
+                in0=dtiles[n][:].rearrange("p t j -> p (t j)"), scalar=0.0,
+                in1=gtiles[n][:].rearrange("p t j -> p (t j)"),
+                op0=ALU.is_gt, op1=ALU.mult)
+            gmtiles[n] = gm
+
+        def v_product(n):
+            gi, gj = seq[n]
+            w = stream.tile([P, T, KP], F32, name="w", tag="w", bufs=2)
+            for t in range(T):
+                col = (gi * T + t) * G + gj
+                nc.vector.scalar_tensor_tensor(
+                    out=w[:, t, :].rearrange("p (u q) -> p u q", u=T),
+                    in0=etiles[n][:, t, :].rearrange("p (u q) -> p u q", u=T),
+                    scalar=vcol[:, 0:1],
+                    in1=gmtiles[n][:, t, :].rearrange("p (q u) -> p u q", u=T),
+                    op0=ALU.mult, op1=ALU.mult,
+                    accum_out=rpart[:, col:col + 1])
+            wtiles[n] = w
+
+        def pe_transposes(n):
+            gi, gj = seq[n]
+            w = wtiles[n]
+            trs = []
+            for t in range(T):
+                tr = psum.tile([P, T, P], F32, name="tr", tag="tr", bufs=4)
+                for u in range(T):
+                    nc.tensor.transpose(out=tr[:, u, :], in_=w[:, t, u * P:(u + 1) * P], identity=ident[:])
+                trs.append(tr)
+            for t in range(T):
+                for u in range(T):
+                    col = (gj * T + u) * (G * T) + gi * T + t
+                    nc.tensor.matmul(out=cpart[:, col:col + 1], lhsT=w[:, t, u * P:(u + 1) * P],
+                                     rhs=ones_f[:, 0:1], start=True, stop=True)
+            trtiles[n] = trs
+
+        def s_aint(n):
+            ab = stream.tile([P, KP, T], BF16, name="ab", tag="ab", bufs=2, align_bytes=64)
+            nc.scalar.copy(out=ab[:], in_=wtiles[n][:].rearrange("p t j -> p j t"))
+            abtiles[n] = ab
+
+        def s_bout(n):
+            bb = stream.tile([P, T, P, T], BF16, name="bb", tag="bb", bufs=2, align_bytes=64)
+            for t in range(T):
+                nc.scalar.copy(out=bb[:, t], in_=trtiles[n][t][:].rearrange("p u c -> p c u"))
+            bbtiles[n] = bb
+
+        def v_quant(n):
+            sa = free_a.pop(0)
+            sb = free_b.pop(0)
+            slot_a[n] = sa
+            slot_b[n] = sb
+            ac = codes.tile([P, KP], U32, name="ac%d" % sa, tag="ac%d" % sa, align_bytes=64)
+            asc = codes.tile([P, KP], U8, name="as%d" % sa, tag="as%d" % sa, align_bytes=64)
+            bc = codes.tile([P, KP], U32, name="bc%d" % sb, tag="bc%d" % sb, align_bytes=64)
+            bsc = codes.tile([P, KP], U8, name="bs%d" % sb, tag="bs%d" % sb, align_bytes=64)
+            nc.vector.quantize_mx(out=ac[:].bitcast(E5), scales=asc[:],
+                                  in_=abtiles[n][:].rearrange("p j t -> p (j t)"))
+            nc.vector.quantize_mx(out=bc[:].bitcast(E5), scales=bsc[:],
+                                  in_=bbtiles[n][:].rearrange("p t c u -> p (t c u)"))
+            acodes[seq[n]] = (ac, asc)
+            bcodes[seq[n]] = (bc, bsc)
+
+        xstage = {}
+
+        def v_xcopy(which, g):
+            st = stream.tile([P, D, T], BF16, name="xst", tag="xst", bufs=1, align_bytes=64)
+            src = x2n if which == 2 else xn
+            nc.vector.tensor_copy(out=st[:], in_=src[:, g].rearrange("p t k -> p k t"))
+            xstage[(which, g)] = st
+
+        def v_xquant(which, g):
+            c_, s_ = (x2c, x2s) if which == 2 else (xc, xs)
+            nc.vector.quantize_mx(out=c_[:, g, :].bitcast(E4), scales=s_[:, g, :],
+                                  in_=xstage[(which, g)][:].rearrange("p k t -> p (k t)"))
+
+        def pe_job(job):
+            kind, g, t = job
+            acc = psum.tile([P, D], F32, name="acc", tag="mx", bufs=3)
+            for h in range(G):
+                if kind == 0:
+                    lc, ls = bcodes[(g, h)]
+                    rc, rsc = x2c, x2s
+                else:
+                    lc, ls = acodes[(h, g)]
+                    rc, rsc = xc, xs
+                nc.tensor.matmul_mx(
+                    out=acc[:],
+                    lhsT=lc[:, t * P:(t + 1) * P].bitcast(E5), lhsT_scale=ls[:, t * P:(t + 1) * P],
+                    rhs=rc[:, h, :].bitcast(E4), rhs_scale=rsc[:, h, :],
+                    start=(h == 0), stop=(h == G - 1))
+            return acc
+
+        def v_epilogue(job, acc):
+            kind, g, t = job
+            src, sums, dst = (xn, rs, o0v) if kind == 0 else (x2n, cs, o1v)
+            z = stream.tile([P, D], F32, name="z", tag="z", bufs=2)
+            o = stream.tile([P, D], F32, name="o", tag="o", bufs=3)
+            nc.vector.scalar_tensor_tensor(out=z[:], in0=src[:, g, t, :], scalar=sums[:, g * T + t:g * T + t + 1],
+                                           in1=acc[:], op0=ALU.mult, op1=ALU.subtract)
+            nc.vector.tensor_tensor(out=o[:], in0=z[:], in1=nil2[:], op=ALU.mult)
+            nc.sync.dma_start(out=dst[:, g, t, :], in_=o[:])
+
+        done_rows = [0] * G
+        done_cols = [0] * G
+
+        for s in range(nb + 2):
+            if s + 2 < nb:
+                load(s + 2)
+            if s < 2:
+                load_x(2, s + 2)
+            elif s < 6:
+                load_x(1, s - 2)
+            if s < nb:
+                s_exp(s)
+            jobs = []
+            if s >= 2:
+                n = s - 2
+                v_quant(n)
+                gi, gj = seq[n]
+                done_rows[gi] += 1
+                done_cols[gj] += 1
+                if done_rows[gi] == G:
+                    jobs.extend([(0, gi, t) for t in range(T)])
+                if done_cols[gj] == G:
+                    jobs.extend([(1, gj, t) for t in range(T)])
+            xwork = None
+            if s < 4:
+                xwork = (2, s)
+            elif s < 8:
+                xwork = (1, s - 4)
+            if xwork is not None:
+                v_xcopy(xwork[0], xwork[1])
+            if s < nb:
+                v_mask(s)
+            if 1 <= s <= nb:
+                pe_transposes(s - 1)
+                s_aint(s - 1)
+                s_bout(s - 1)
+            if s < nb:
+                v_product(s)
+            if xwork is not None:
+                v_xquant(xwork[0], xwork[1])
+            for job in jobs:
+                kind, g, t = job
+                if t == 0:
+                    if kind == 0:
+                        nc.vector.tensor_reduce(out=rs[:, g * T:(g + 1) * T],
+                                                in_=rpart[:, g * T * G:(g + 1) * T * G].rearrange("p (t n) -> p t n", n=G),
+                                                axis=AX.X, op=ALU.add)
+                    else:
+                        nc.vector.tensor_reduce(out=cs[:, g * T:(g + 1) * T],
+                                                in_=cpart[:, g * T * G * T:(g + 1) * T * G * T].rearrange("p (t n) -> p t n", n=G * T),
+                                                axis=AX.X, op=ALU.add)
+            accs = []
+            for i in range(len(jobs)):
+                accs.append(pe_job(jobs[i]))
+                if i >= 2:
+                    v_epilogue(jobs[i - 2], accs[i - 2])
+            for i in range(max(0, len(jobs) - 2), len(jobs)):
+                v_epilogue(jobs[i], accs[i])
+            for job in jobs:
+                kind, g, t = job
+                if t == T - 1:
+                    for n in range(nb):
+                        if kind == 0 and seq[n][0] == g:
+                            free_b.append(slot_b[n])
+                            free_b.sort()
+                        if kind == 1 and seq[n][1] == g:
+                            free_a.append(slot_a[n])
+                            free_a.sort()

@@ -15,6 +15,9 @@ ALU = mybir.AluOpType
 ACT = mybir.ActivationFunctionType
 AX = mybir.AxisListType
 
+XINT_S = ()
+CSUM_S = True
+AINT_V = (15,)
 P = 128
 G = 4
 T = 4
@@ -53,17 +56,20 @@ def tile_rbf_t_v_kernel(tc, X, X2, lengthscale, variance, d2, grad_out, out_0, o
 
         prow = const.tile([P, 544], BF16, name="prow")
         ones_bf = const.tile([P, P], BF16, name="ones_bf")
-        ones_f = const.tile([P, 8], F32, name="ones_f")
         ident = const.tile([P, P], F32, name="ident")
         nc.gpsimd.memset(prow[:], 0.0)
         nc.gpsimd.memset(ones_bf[:], 1.0)
-        nc.gpsimd.memset(ones_f[:], 1.0)
         make_identity(nc, ident[:])
         nc.sync.dma_start(out=prow[0:1, 0:D], in_=lengthscale)
         nc.sync.dma_start(out=prow[0:1, D:D + 1], in_=variance.rearrange("(o k) -> o k", o=1))
 
-        xn = const.tile([P, G, T, D], BF16, name="xn")
-        x2n = const.tile([P, G, T, D], BF16, name="x2n")
+        xn = []
+        x2n = []
+        for g in range(G):
+            xg = const.tile([P, T, D], BF16, name="xn%d" % g)
+            x2g = const.tile([P, T, D], BF16, name="x2n%d" % g)
+            xn.append(xg)
+            x2n.append(x2g)
         xc = const.tile([P, G, D], U32, name="xc", align_bytes=64)
         xs = const.tile([P, G, D], U8, name="xs", align_bytes=64)
         x2c = const.tile([P, G, D], U32, name="x2c", align_bytes=64)
@@ -71,7 +77,7 @@ def tile_rbf_t_v_kernel(tc, X, X2, lengthscale, variance, d2, grad_out, out_0, o
         rpart = const.tile([P, G * T * G], F32, name="rpart")
         rs = const.tile([P, G * T], F32, name="rs")
         cs = const.tile([P, G * T], F32, name="cs")
-        cpart = psum.tile([P, G * T * G * T], F32, name="cpart", tag="cpart")
+        cpart = const.tile([P, G, T, G], F32, name="cpart")
 
         dtiles = {}
         gtiles = {}
@@ -87,17 +93,19 @@ def tile_rbf_t_v_kernel(tc, X, X2, lengthscale, variance, d2, grad_out, out_0, o
 
         def load_x(which, g):
             if which == 2:
-                nc.sync.dma_start(out=x2n[:, g], in_=x2v[:, g])
+                nc.sync.dma_start(out=x2n[g][:], in_=x2v[:, g])
             else:
-                nc.sync.dma_start(out=xn[:, g], in_=xv[:, g])
+                nc.sync.dma_start(out=xn[g][:], in_=xv[:, g])
 
         load(0)
         load_x(2, 0)
         load(1)
         load_x(2, 1)
+        load_x(2, 2)
+        load_x(2, 3)
 
-        pb1 = psum.tile([P, D], F32, name="pb1", tag="mx", bufs=3)
-        pb2 = psum.tile([P, D], F32, name="pb2", tag="mx", bufs=3)
+        pb1 = psum.tile([P, D], F32, name="pb1", tag="mx", bufs=2)
+        pb2 = psum.tile([P, D], F32, name="pb2", tag="mx", bufs=2)
         nc.tensor.matmul(out=pb1[:], lhsT=ones_bf[:], rhs=prow[:, 0:D], start=True, stop=True)
         nc.tensor.matmul(out=pb2[:, 0:32], lhsT=ones_bf[:], rhs=prow[:, D:D + 32], start=True, stop=True)
         x32 = const.tile([P, 544], F32, name="x32")
@@ -110,16 +118,21 @@ def tile_rbf_t_v_kernel(tc, X, X2, lengthscale, variance, d2, grad_out, out_0, o
         nc.vector.scalar_tensor_tensor(out=na[:], in0=x32[:], scalar=-1.0, in1=x32[:], op0=ALU.mult, op1=ALU.min)
         nc.scalar.activation(out=na[:], in_=na[:], func=ACT.Exp)
         nc.scalar.activation(out=na[:], in_=na[:], func=ACT.Ln, bias=1.0)
-        nc.vector.scalar_tensor_tensor(out=sp[:], in0=x32[:], scalar=0.0, in1=na[:], op0=ALU.max, op1=ALU.add)
-        nc.vector.tensor_copy(out=vcol[:, 0:1], in_=sp[:, D:D + 1])
-        nc.vector.tensor_tensor(out=x32[:, 0:D], in0=sp[:, 0:D], in1=sp[:, 0:D], op=ALU.mult)
-        nc.vector.reciprocal(out=na[:, 0:D], in_=x32[:, 0:D])
-        nc.vector.tensor_scalar(out=nil2[:], in0=na[:, 0:D], scalar1=-1.0, scalar2=None, op0=ALU.mult)
+
+        def params_v():
+            nc.vector.scalar_tensor_tensor(out=sp[:], in0=x32[:], scalar=0.0, in1=na[:], op0=ALU.max, op1=ALU.add)
+            nc.vector.tensor_copy(out=vcol[:, 0:1], in_=sp[:, D:D + 1])
+
+        def params_l():
+            nc.vector.tensor_tensor(out=x32[:, 0:D], in0=sp[:, 0:D], in1=sp[:, 0:D], op=ALU.mult)
+            nc.vector.reciprocal(out=na[:, 0:D], in_=x32[:, 0:D])
+            nc.vector.tensor_scalar(out=nil2[:], in0=na[:, 0:D], scalar1=-1.0, scalar2=None, op0=ALU.mult)
 
         etiles = {}
         gmtiles = {}
         wtiles = {}
         trtiles = {}
+        smtiles = {}
         abtiles = {}
         bbtiles = {}
         acodes = {}
@@ -169,16 +182,31 @@ def tile_rbf_t_v_kernel(tc, X, X2, lengthscale, variance, d2, grad_out, out_0, o
                 for u in range(T):
                     nc.tensor.transpose(out=tr[:, u, :], in_=w[:, t, u * P:(u + 1) * P], identity=ident[:])
                 trs.append(tr)
-            for t in range(T):
-                for u in range(T):
-                    col = (gj * T + u) * (G * T) + gi * T + t
-                    nc.tensor.matmul(out=cpart[:, col:col + 1], lhsT=w[:, t, u * P:(u + 1) * P],
-                                     rhs=ones_f[:, 0:1], start=True, stop=True)
+            sm = psum.tile([P, T, P], F32, name="sm", tag="sm", bufs=2)
+            for u in range(T):
+                for t in range(T):
+                    nc.tensor.matmul(out=sm[:, u, :], lhsT=w[:, t, u * P:(u + 1) * P], rhs=ident[:],
+                                     start=(t == 0), stop=(t == T - 1), is_transpose=True)
             trtiles[n] = trs
+            smtiles[n] = sm
+
+        def v_csum(n):
+            gi, gj = seq[n]
+            nc.vector.tensor_reduce(out=cpart[:, gj, :, gi], in_=smtiles[n][:], axis=AX.X, op=ALU.add)
+
+        def s_csum(n):
+            gi, gj = seq[n]
+            junk = stream.tile([P, T, P], BF16, name="junk", tag="junk", bufs=1)
+            for u in range(T):
+                nc.scalar.activation(out=junk[:, u, :], in_=smtiles[n][:, u, :], func=ACT.Copy,
+                                     accum_out=cpart[:, gj, u, gi:gi + 1])
 
         def s_aint(n):
             ab = stream.tile([P, KP, T], BF16, name="ab", tag="ab", bufs=2, align_bytes=64)
-            nc.scalar.copy(out=ab[:], in_=wtiles[n][:].rearrange("p t j -> p j t"))
+            if n in AINT_V:
+                nc.vector.tensor_copy(out=ab[:], in_=wtiles[n][:].rearrange("p t j -> p j t"))
+            else:
+                nc.scalar.copy(out=ab[:], in_=wtiles[n][:].rearrange("p t j -> p j t"))
             abtiles[n] = ab
 
         def s_bout(n):
@@ -206,9 +234,12 @@ def tile_rbf_t_v_kernel(tc, X, X2, lengthscale, variance, d2, grad_out, out_0, o
         xstage = {}
 
         def v_xcopy(which, g):
-            st = stream.tile([P, D, T], BF16, name="xst", tag="xst", bufs=1, align_bytes=64)
+            st = stream.tile([P, D, T], BF16, name="xst", tag="xst", bufs=2, align_bytes=64)
             src = x2n if which == 2 else xn
-            nc.vector.tensor_copy(out=st[:], in_=src[:, g].rearrange("p t k -> p k t"))
+            if (which, g) in XINT_S:
+                nc.scalar.copy(out=st[:], in_=src[g][:].rearrange("p t k -> p k t"))
+            else:
+                nc.vector.tensor_copy(out=st[:], in_=src[g][:].rearrange("p t k -> p k t"))
             xstage[(which, g)] = st
 
         def v_xquant(which, g):
@@ -218,7 +249,7 @@ def tile_rbf_t_v_kernel(tc, X, X2, lengthscale, variance, d2, grad_out, out_0, o
 
         def pe_job(job):
             kind, g, t = job
-            acc = psum.tile([P, D], F32, name="acc", tag="mx", bufs=3)
+            acc = psum.tile([P, D], F32, name="acc", tag="mx", bufs=2)
             for h in range(G):
                 if kind == 0:
                     lc, ls = bcodes[(g, h)]
@@ -237,8 +268,8 @@ def tile_rbf_t_v_kernel(tc, X, X2, lengthscale, variance, d2, grad_out, out_0, o
             kind, g, t = job
             src, sums, dst = (xn, rs, o0v) if kind == 0 else (x2n, cs, o1v)
             z = stream.tile([P, D], F32, name="z", tag="z", bufs=2)
-            o = stream.tile([P, D], F32, name="o", tag="o", bufs=3)
-            nc.vector.scalar_tensor_tensor(out=z[:], in0=src[:, g, t, :], scalar=sums[:, g * T + t:g * T + t + 1],
+            o = stream.tile([P, D], F32, name="o", tag="o", bufs=5)
+            nc.vector.scalar_tensor_tensor(out=z[:], in0=src[g][:, t, :], scalar=sums[:, g * T + t:g * T + t + 1],
                                            in1=acc[:], op0=ALU.mult, op1=ALU.subtract)
             nc.vector.tensor_tensor(out=o[:], in0=z[:], in1=nil2[:], op=ALU.mult)
             nc.sync.dma_start(out=dst[:, g, t, :], in_=o[:])
@@ -249,16 +280,16 @@ def tile_rbf_t_v_kernel(tc, X, X2, lengthscale, variance, d2, grad_out, out_0, o
         for s in range(nb + 2):
             if s + 2 < nb:
                 load(s + 2)
-            if s < 2:
-                load_x(2, s + 2)
-            elif s < 6:
-                load_x(1, s - 2)
+            if s < 4:
+                load_x(1, s)
             if s < nb:
                 s_exp(s)
             jobs = []
             if s >= 2:
                 n = s - 2
                 v_quant(n)
+                if not CSUM_S:
+                    v_csum(n)
                 gi, gj = seq[n]
                 done_rows[gi] += 1
                 done_cols[gj] += 1
@@ -266,23 +297,24 @@ def tile_rbf_t_v_kernel(tc, X, X2, lengthscale, variance, d2, grad_out, out_0, o
                     jobs.extend([(0, gi, t) for t in range(T)])
                 if done_cols[gj] == G:
                     jobs.extend([(1, gj, t) for t in range(T)])
-            xwork = None
-            if s < 4:
-                xwork = (2, s)
-            elif s < 8:
-                xwork = (1, s - 4)
-            if xwork is not None:
-                v_xcopy(xwork[0], xwork[1])
+            if 1 <= s <= 8:
+                v_xquant(2 if s <= 4 else 1, (s - 1) % 4)
             if s < nb:
                 v_mask(s)
+            if s == 0:
+                params_v()
             if 1 <= s <= nb:
                 pe_transposes(s - 1)
                 s_aint(s - 1)
                 s_bout(s - 1)
+                if CSUM_S:
+                    s_csum(s - 1)
             if s < nb:
                 v_product(s)
-            if xwork is not None:
-                v_xquant(xwork[0], xwork[1])
+            if s == 0:
+                params_l()
+            if s < 8:
+                v_xcopy(2 if s < 4 else 1, s % 4)
             for job in jobs:
                 kind, g, t = job
                 if t == 0:
@@ -292,15 +324,15 @@ def tile_rbf_t_v_kernel(tc, X, X2, lengthscale, variance, d2, grad_out, out_0, o
                                                 axis=AX.X, op=ALU.add)
                     else:
                         nc.vector.tensor_reduce(out=cs[:, g * T:(g + 1) * T],
-                                                in_=cpart[:, g * T * G * T:(g + 1) * T * G * T].rearrange("p (t n) -> p t n", n=G * T),
+                                                in_=cpart[:, g],
                                                 axis=AX.X, op=ALU.add)
             accs = []
             for i in range(len(jobs)):
                 accs.append(pe_job(jobs[i]))
-                if i >= 2:
-                    v_epilogue(jobs[i - 2], accs[i - 2])
-            for i in range(max(0, len(jobs) - 2), len(jobs)):
-                v_epilogue(jobs[i], accs[i])
+                if i >= 1:
+                    v_epilogue(jobs[i - 1], accs[i - 1])
+            if len(jobs) > 0:
+                v_epilogue(jobs[len(jobs) - 1], accs[len(jobs) - 1])
             for job in jobs:
                 kind, g, t = job
                 if t == T - 1:

@@ -48,7 +48,6 @@ def tile_rbf_t_v_kernel(tc, X, X2, lengthscale, variance, d2, grad_out, out_0, o
     o1v = out_1.rearrange("(g p t) k -> p g t k", p=P, t=T)
 
     with ExitStack() as ctx:
-        ctx.enter_context(tc.manual_schedule())
         const = ctx.enter_context(tc.tile_pool(name="const", bufs=1))
         stream = ctx.enter_context(tc.tile_pool(name="stream", bufs=2))
         codes = ctx.enter_context(tc.tile_pool(name="codes", bufs=1))
@@ -145,8 +144,8 @@ def tile_rbf_t_v_kernel(tc, X, X2, lengthscale, variance, d2, grad_out, out_0, o
         def s_exp(n):
             e = stream.tile([P, T, KP], F32, name="e", tag="e", bufs=2)
             nc.scalar.activation(
-                out=e[:].rearrange("p t (u q) -> p t u q", u=T),
-                in_=dtiles[n][:].rearrange("p t (q u) -> p t u q", u=T),
+                out=e[:].rearrange("p t j -> p (t j)"),
+                in_=dtiles[n][:].rearrange("p t j -> p (t j)"),
                 func=ACT.Exp, scale=-0.5)
             etiles[n] = e
 
@@ -165,10 +164,10 @@ def tile_rbf_t_v_kernel(tc, X, X2, lengthscale, variance, d2, grad_out, out_0, o
             for t in range(T):
                 col = (gi * T + t) * G + gj
                 nc.vector.scalar_tensor_tensor(
-                    out=w[:, t, :].rearrange("p (u q) -> p u q", u=T),
-                    in0=etiles[n][:, t, :].rearrange("p (u q) -> p u q", u=T),
+                    out=w[:, t, :].rearrange("p (u q) -> p q u", u=T),
+                    in0=etiles[n][:, t, :].rearrange("p (q u) -> p q u", u=T),
                     scalar=vcol[:, 0:1],
-                    in1=gmtiles[n][:, t, :].rearrange("p (q u) -> p u q", u=T),
+                    in1=gmtiles[n][:, t, :].rearrange("p (q u) -> p q u", u=T),
                     op0=ALU.mult, op1=ALU.mult,
                     accum_out=rpart[:, col:col + 1])
             wtiles[n] = w

@@ -15,9 +15,12 @@ ALU = mybir.AluOpType
 ACT = mybir.ActivationFunctionType
 AX = mybir.AxisListType
 
-XINT_S = ()
+XINT_S = ((1, 1), (1, 2), (1, 3))
 CSUM_S = True
-AINT_V = (15,)
+TRB = 4
+SMB = 1
+MXB = 3
+AINT_V = ()
 P = 128
 G = 4
 T = 4
@@ -53,14 +56,12 @@ def tile_rbf_t_v_kernel(tc, X, X2, lengthscale, variance, d2, grad_out, out_0, o
         codes = ctx.enter_context(tc.tile_pool(name="codes", bufs=1))
         psum = ctx.enter_context(tc.psum_pool(name="psum", bufs=1))
 
-        prow = const.tile([P, 544], BF16, name="prow")
-        ones_bf = const.tile([P, P], BF16, name="ones_bf")
         ident = const.tile([P, P], F32, name="ident")
-        nc.gpsimd.memset(prow[:], 0.0)
-        nc.gpsimd.memset(ones_bf[:], 1.0)
         make_identity(nc, ident[:])
-        nc.sync.dma_start(out=prow[0:1, 0:D], in_=lengthscale)
-        nc.sync.dma_start(out=prow[0:1, D:D + 1], in_=variance.rearrange("(o k) -> o k", o=1))
+        lsb = const.tile([P, T], BF16, name="lsb")
+        vb = const.tile([P, 1], BF16, name="vb")
+        nc.scalar.dma_start(out=lsb[:], in_=lengthscale.rearrange("o (p c) -> (o p) c", c=T))
+        nc.scalar.dma_start(out=vb[:], in_=variance.partition_broadcast(P))
 
         xn = []
         x2n = []
@@ -103,29 +104,31 @@ def tile_rbf_t_v_kernel(tc, X, X2, lengthscale, variance, d2, grad_out, out_0, o
         load_x(2, 2)
         load_x(2, 3)
 
-        pb1 = psum.tile([P, D], F32, name="pb1", tag="mx", bufs=2)
-        pb2 = psum.tile([P, D], F32, name="pb2", tag="mx", bufs=2)
-        nc.tensor.matmul(out=pb1[:], lhsT=ones_bf[:], rhs=prow[:, 0:D], start=True, stop=True)
-        nc.tensor.matmul(out=pb2[:, 0:32], lhsT=ones_bf[:], rhs=prow[:, D:D + 32], start=True, stop=True)
-        x32 = const.tile([P, 544], F32, name="x32")
-        na = const.tile([P, 544], F32, name="na")
-        sp = const.tile([P, 544], F32, name="sp")
+        x5 = const.tile([P, 8], F32, name="x5")
+        na = const.tile([P, 8], F32, name="na")
+        rl = const.tile([P, 8], F32, name="rl")
+        sp = const.tile([P, 8], F32, name="sp")
+        sq = const.tile([P, 8], F32, name="sq")
+        nil2c = const.tile([P, 8], F32, name="nil2c")
         nil2 = const.tile([P, D], F32, name="nil2")
-        vcol = const.tile([P, 8], F32, name="vcol")
-        nc.vector.tensor_copy(out=x32[:, 0:D], in_=pb1[:])
-        nc.vector.tensor_copy(out=x32[:, D:D + 32], in_=pb2[:, 0:32])
-        nc.vector.scalar_tensor_tensor(out=na[:], in0=x32[:], scalar=-1.0, in1=x32[:], op0=ALU.mult, op1=ALU.min)
-        nc.scalar.activation(out=na[:], in_=na[:], func=ACT.Exp)
-        nc.scalar.activation(out=na[:], in_=na[:], func=ACT.Ln, bias=1.0)
-
-        def params_v():
-            nc.vector.scalar_tensor_tensor(out=sp[:], in0=x32[:], scalar=0.0, in1=na[:], op0=ALU.max, op1=ALU.add)
-            nc.vector.tensor_copy(out=vcol[:, 0:1], in_=sp[:, D:D + 1])
+        nc.vector.tensor_copy(out=x5[:, 0:T], in_=lsb[:])
+        nc.vector.tensor_copy(out=x5[:, T:T + 1], in_=vb[:])
+        nc.vector.scalar_tensor_tensor(out=na[:, 0:5], in0=x5[:, 0:5], scalar=-1.0, in1=x5[:, 0:5], op0=ALU.mult, op1=ALU.min)
+        nc.vector.tensor_scalar(out=rl[:, 0:5], in0=x5[:, 0:5], scalar1=0.0, scalar2=None, op0=ALU.max)
+        nc.scalar.activation(out=na[:, 0:5], in_=na[:, 0:5], func=ACT.Exp)
+        nc.scalar.activation(out=na[:, 0:5], in_=na[:, 0:5], func=ACT.Ln, bias=1.0)
+        nc.vector.tensor_tensor(out=sp[:, 0:5], in0=na[:, 0:5], in1=rl[:, 0:5], op=ALU.add)
+        vcol = sp[:, T:T + 1]
 
         def params_l():
-            nc.vector.tensor_tensor(out=x32[:, 0:D], in0=sp[:, 0:D], in1=sp[:, 0:D], op=ALU.mult)
-            nc.vector.reciprocal(out=na[:, 0:D], in_=x32[:, 0:D])
-            nc.vector.tensor_scalar(out=nil2[:], in0=na[:, 0:D], scalar1=-1.0, scalar2=None, op0=ALU.mult)
+            nc.vector.tensor_tensor(out=sq[:, 0:T], in0=sp[:, 0:T], in1=sp[:, 0:T], op=ALU.mult)
+            nc.vector.reciprocal(out=sq[:, 0:T], in_=sq[:, 0:T])
+            nc.vector.tensor_scalar(out=nil2c[:, 0:T], in0=sq[:, 0:T], scalar1=-1.0, scalar2=None, op0=ALU.mult)
+            pb = psum.tile([P, D], F32, name="pb", tag="mx", bufs=MXB)
+            for c in range(T):
+                nc.tensor.matmul(out=pb[:, c * P:(c + 1) * P], lhsT=nil2c[:, c:c + 1].to_broadcast([P, P]), rhs=ident[:],
+                                 start=True, stop=True)
+            nc.scalar.copy(out=nil2[:].rearrange("p (n c) -> p n c", c=T), in_=pb[:].rearrange("p (c n) -> p n c", c=T))
 
         etiles = {}
         gmtiles = {}
@@ -166,7 +169,7 @@ def tile_rbf_t_v_kernel(tc, X, X2, lengthscale, variance, d2, grad_out, out_0, o
                 nc.vector.scalar_tensor_tensor(
                     out=w[:, t, :].rearrange("p (u q) -> p q u", u=T),
                     in0=etiles[n][:, t, :].rearrange("p (q u) -> p q u", u=T),
-                    scalar=vcol[:, 0:1],
+                    scalar=vcol,
                     in1=gmtiles[n][:, t, :].rearrange("p (q u) -> p q u", u=T),
                     op0=ALU.mult, op1=ALU.mult,
                     accum_out=rpart[:, col:col + 1])
@@ -177,11 +180,11 @@ def tile_rbf_t_v_kernel(tc, X, X2, lengthscale, variance, d2, grad_out, out_0, o
             w = wtiles[n]
             trs = []
             for t in range(T):
-                tr = psum.tile([P, T, P], F32, name="tr", tag="tr", bufs=4)
+                tr = psum.tile([P, T, P], F32, name="tr", tag="tr", bufs=TRB)
                 for u in range(T):
                     nc.tensor.transpose(out=tr[:, u, :], in_=w[:, t, u * P:(u + 1) * P], identity=ident[:])
                 trs.append(tr)
-            sm = psum.tile([P, T, P], F32, name="sm", tag="sm", bufs=2)
+            sm = psum.tile([P, T, P], F32, name="sm", tag="sm", bufs=SMB)
             for u in range(T):
                 for t in range(T):
                     nc.tensor.matmul(out=sm[:, u, :], lhsT=w[:, t, u * P:(u + 1) * P], rhs=ident[:],
@@ -248,7 +251,7 @@ def tile_rbf_t_v_kernel(tc, X, X2, lengthscale, variance, d2, grad_out, out_0, o
 
         def pe_job(job):
             kind, g, t = job
-            acc = psum.tile([P, D], F32, name="acc", tag="mx", bufs=2)
+            acc = psum.tile([P, D], F32, name="acc", tag="mx", bufs=MXB)
             for h in range(G):
                 if kind == 0:
                     lc, ls = bcodes[(g, h)]
@@ -263,13 +266,18 @@ def tile_rbf_t_v_kernel(tc, X, X2, lengthscale, variance, d2, grad_out, out_0, o
                     start=(h == 0), stop=(h == G - 1))
             return acc
 
-        def v_epilogue(job, acc):
+        def v_epi1(job, acc):
             kind, g, t = job
-            src, sums, dst = (xn, rs, o0v) if kind == 0 else (x2n, cs, o1v)
-            z = stream.tile([P, D], F32, name="z", tag="z", bufs=2)
-            o = stream.tile([P, D], F32, name="o", tag="o", bufs=5)
+            src, sums = (xn, rs) if kind == 0 else (x2n, cs)
+            z = stream.tile([P, D], F32, name="z", tag="z", bufs=4)
             nc.vector.scalar_tensor_tensor(out=z[:], in0=src[g][:, t, :], scalar=sums[:, g * T + t:g * T + t + 1],
                                            in1=acc[:], op0=ALU.mult, op1=ALU.subtract)
+            return z
+
+        def v_epi2(job, z):
+            kind, g, t = job
+            dst = o0v if kind == 0 else o1v
+            o = stream.tile([P, D], F32, name="o", tag="o", bufs=4)
             nc.vector.tensor_tensor(out=o[:], in0=z[:], in1=nil2[:], op=ALU.mult)
             nc.sync.dma_start(out=dst[:, g, t, :], in_=o[:])
 
@@ -298,10 +306,10 @@ def tile_rbf_t_v_kernel(tc, X, X2, lengthscale, variance, d2, grad_out, out_0, o
                     jobs.extend([(1, gj, t) for t in range(T)])
             if 1 <= s <= 8:
                 v_xquant(2 if s <= 4 else 1, (s - 1) % 4)
-            if s < nb:
-                v_mask(s)
             if s == 0:
-                params_v()
+                v_mask(0)
+            if s + 1 < nb:
+                v_mask(s + 1)
             if 1 <= s <= nb:
                 pe_transposes(s - 1)
                 s_aint(s - 1)
@@ -325,13 +333,13 @@ def tile_rbf_t_v_kernel(tc, X, X2, lengthscale, variance, d2, grad_out, out_0, o
                         nc.vector.tensor_reduce(out=cs[:, g * T:(g + 1) * T],
                                                 in_=cpart[:, g],
                                                 axis=AX.X, op=ALU.add)
-            accs = []
-            for i in range(len(jobs)):
-                accs.append(pe_job(jobs[i]))
-                if i >= 1:
-                    v_epilogue(jobs[i - 1], accs[i - 1])
-            if len(jobs) > 0:
-                v_epilogue(jobs[len(jobs) - 1], accs[len(jobs) - 1])
+            for i in range(0, len(jobs), 2):
+                acc_a = pe_job(jobs[i])
+                acc_b = pe_job(jobs[i + 1])
+                z_a = v_epi1(jobs[i], acc_a)
+                z_b = v_epi1(jobs[i + 1], acc_b)
+                v_epi2(jobs[i], z_a)
+                v_epi2(jobs[i + 1], z_b)
             for job in jobs:
                 kind, g, t = job
                 if t == T - 1:

@@ -15,7 +15,7 @@ ALU = mybir.AluOpType
 ACT = mybir.ActivationFunctionType
 AX = mybir.AxisListType
 
-XINT_S = ((1, 1), (1, 2), (1, 3))
+XINT_S = ((1, 0), (1, 1), (1, 2), (1, 3))
 CSUM_S = True
 TRB = 4
 SMB = 1
@@ -84,6 +84,19 @@ def tile_rbf_t_v_kernel(tc, X, X2, lengthscale, variance, d2, grad_out, out_0, o
 
         def load(n):
             gi, gj = seq[n]
+            if n == 0:
+                dl = []
+                gl = []
+                for t in range(T):
+                    d0 = const.tile([P, KP], F32, name="d0_%d" % t)
+                    g0 = const.tile([P, KP], BF16, name="g0_%d" % t)
+                    nc.sync.dma_start(out=d0[:], in_=d2v[:, gi, t, gj * KP:(gj + 1) * KP])
+                    nc.sync.dma_start(out=g0[:], in_=gv[:, gi, t, gj * KP:(gj + 1) * KP])
+                    dl.append(d0)
+                    gl.append(g0)
+                dtiles[n] = dl
+                gtiles[n] = gl
+                return
             dt_ = stream.tile([P, T, KP], F32, name="dt_", tag="dt", bufs=3)
             gt_ = stream.tile([P, T, KP], BF16, name="gt_", tag="gt", bufs=3)
             nc.sync.dma_start(out=dt_[:], in_=d2v[:, gi, :, gj * KP:(gj + 1) * KP])
@@ -146,6 +159,11 @@ def tile_rbf_t_v_kernel(tc, X, X2, lengthscale, variance, d2, grad_out, out_0, o
 
         def s_exp(n):
             e = stream.tile([P, T, KP], F32, name="e", tag="e", bufs=2)
+            etiles[n] = e
+            if n == 0:
+                for t in range(T):
+                    nc.scalar.activation(out=e[:, t, :], in_=dtiles[n][t][:], func=ACT.Exp, scale=-0.5)
+                return
             nc.scalar.activation(
                 out=e[:].rearrange("p t j -> p (t j)"),
                 in_=dtiles[n][:].rearrange("p t j -> p (t j)"),
@@ -154,6 +172,12 @@ def tile_rbf_t_v_kernel(tc, X, X2, lengthscale, variance, d2, grad_out, out_0, o
 
         def v_mask(n):
             gm = stream.tile([P, T, KP], BF16, name="gm", tag="gm", bufs=2)
+            gmtiles[n] = gm
+            if n == 0:
+                for t in range(T):
+                    nc.vector.scalar_tensor_tensor(out=gm[:, t, :], in0=dtiles[n][t][:], scalar=0.0, in1=gtiles[n][t][:],
+                                                   op0=ALU.is_gt, op1=ALU.mult)
+                return
             nc.vector.scalar_tensor_tensor(
                 out=gm[:].rearrange("p t j -> p (t j)"),
                 in0=dtiles[n][:].rearrange("p t j -> p (t j)"), scalar=0.0,
@@ -205,10 +229,8 @@ def tile_rbf_t_v_kernel(tc, X, X2, lengthscale, variance, d2, grad_out, out_0, o
 
         def s_aint(n):
             ab = stream.tile([P, KP, T], BF16, name="ab", tag="ab", bufs=2, align_bytes=64)
-            if n in AINT_V:
-                nc.vector.tensor_copy(out=ab[:], in_=wtiles[n][:].rearrange("p t j -> p j t"))
-            else:
-                nc.scalar.copy(out=ab[:], in_=wtiles[n][:].rearrange("p t j -> p j t"))
+            nc.scalar.copy(out=ab[:].rearrange("p (c i) t -> p c t i", i=4),
+                           in_=wtiles[n][:].rearrange("p t (c i) -> p c t i", i=4))
             abtiles[n] = ab
 
         def s_bout(n):
@@ -239,9 +261,11 @@ def tile_rbf_t_v_kernel(tc, X, X2, lengthscale, variance, d2, grad_out, out_0, o
             st = stream.tile([P, D, T], BF16, name="xst", tag="xst", bufs=2, align_bytes=64)
             src = x2n if which == 2 else xn
             if (which, g) in XINT_S:
-                nc.scalar.copy(out=st[:], in_=src[g][:].rearrange("p t k -> p k t"))
+                nc.scalar.copy(out=st[:].rearrange("p (c i) t -> p c t i", i=4),
+                               in_=src[g][:].rearrange("p t (c i) -> p c t i", i=4))
             else:
-                nc.vector.tensor_copy(out=st[:], in_=src[g][:].rearrange("p t k -> p k t"))
+                nc.vector.tensor_copy(out=st[:].rearrange("p (c i) t -> p c t i", i=4),
+                                      in_=src[g][:].rearrange("p t (c i) -> p c t i", i=4))
             xstage[(which, g)] = st
 
         def v_xquant(which, g):

from contextlib import ExitStack

import concourse.mybir as mybir
from concourse.masks import make_identity

FLOPS = 2 * 2 * 2048 * 2048 * 512

F32 = mybir.dt.float32
BF16 = mybir.dt.bfloat16
U32 = mybir.dt.uint32
U8 = mybir.dt.uint8
E4 = mybir.dt.float8_e4m3fn_x4
E5 = mybir.dt.float8_e5m2_x4
ALU = mybir.AluOpType
ACT = mybir.ActivationFunctionType
AX = mybir.AxisListType

XINT_S = ((1, 0), (1, 1), (1, 2), (1, 3))
CSUM_S = True
TRB = 4
SMB = 1
MXB = 3
AINT_V = ()
P = 128
G = 4
T = 4
KP = 512
D = 512


def block_order():
    seq = []
    for d in range(G):
        for gj in range(d, G):
            seq.append((d, gj))
        for gi in range(d + 1, G):
            seq.append((gi, d))
    return seq


def tile_rbf_t_v_kernel(tc, X, X2, lengthscale, variance, d2, grad_out, out_0, out_1):
    nc = tc.nc
    seq = block_order()
    nb = len(seq)

    d2v = d2.rearrange("(g p t) j -> p g t j", p=P, t=T)
    gv = grad_out.rearrange("(g p t) j -> p g t j", p=P, t=T)
    xv = X.rearrange("(g p t) k -> p g t k", p=P, t=T)
    x2v = X2.rearrange("(g p t) k -> p g t k", p=P, t=T)
    o0v = out_0.rearrange("(g p t) k -> p g t k", p=P, t=T)
    o1v = out_1.rearrange("(g p t) k -> p g t k", p=P, t=T)

    with ExitStack() as ctx:
        const = ctx.enter_context(tc.tile_pool(name="const", bufs=1))
        stream = ctx.enter_context(tc.tile_pool(name="stream", bufs=2))
        codes = ctx.enter_context(tc.tile_pool(name="codes", bufs=1))
        psum = ctx.enter_context(tc.psum_pool(name="psum", bufs=1))

        ident = const.tile([P, P], F32, name="ident")
        make_identity(nc, ident[:])
        lsb = const.tile([P, T], BF16, name="lsb")
        vb = const.tile([P, 1], BF16, name="vb")
        nc.scalar.dma_start(out=lsb[:], in_=lengthscale.rearrange("o (p c) -> (o p) c", c=T))
        nc.scalar.dma_start(out=vb[:], in_=variance.partition_broadcast(P))

        xn = []
        x2n = []
        for g in range(G):
            xg = const.tile([P, T, D], BF16, name="xn%d" % g)
            x2g = const.tile([P, T, D], BF16, name="x2n%d" % g)
            xn.append(xg)
            x2n.append(x2g)
        xc = const.tile([P, G, D], U32, name="xc", align_bytes=64)
        xs = const.tile([P, G, D], U8, name="xs", align_bytes=64)
        x2c = const.tile([P, G, D], U32, name="x2c", align_bytes=64)
        x2s = const.tile([P, G, D], U8, name="x2s", align_bytes=64)
        rpart = const.tile([P, G * T * G], F32, name="rpart")
        rs = const.tile([P, G * T], F32, name="rs")
        cs = const.tile([P, G * T], F32, name="cs")
        cpart = const.tile([P, G, T, G], F32, name="cpart")

        dtiles = {}
        gtiles = {}

        def load(n):
            gi, gj = seq[n]
            if n == 0:
                dl = []
                gl = []
                for t in range(T):
                    d0 = const.tile([P, KP], F32, name="d0_%d" % t)
                    g0 = const.tile([P, KP], BF16, name="g0_%d" % t)
                    nc.sync.dma_start(out=d0[:], in_=d2v[:, gi, t, gj * KP:(gj + 1) * KP])
                    nc.sync.dma_start(out=g0[:], in_=gv[:, gi, t, gj * KP:(gj + 1) * KP])
                    dl.append(d0)
                    gl.append(g0)
                dtiles[n] = dl
                gtiles[n] = gl
                return
            dt_ = stream.tile([P, T, KP], F32, name="dt_", tag="dt", bufs=3)
            gt_ = stream.tile([P, T, KP], BF16, name="gt_", tag="gt", bufs=3)
            nc.sync.dma_start(out=dt_[:], in_=d2v[:, gi, :, gj * KP:(gj + 1) * KP])
            nc.sync.dma_start(out=gt_[:], in_=gv[:, gi, :, gj * KP:(gj + 1) * KP])
            dtiles[n] = dt_
            gtiles[n] = gt_

        def load_x(which, g):
            if which == 2:
                nc.sync.dma_start(out=x2n[g][:], in_=x2v[:, g])
            else:
                nc.sync.dma_start(out=xn[g][:], in_=xv[:, g])

        load(0)
        load_x(2, 0)
        load(1)
        load_x(2, 1)
        load_x(2, 2)
        load_x(2, 3)

        x5 = const.tile([P, 8], F32, name="x5")
        na = const.tile([P, 8], F32, name="na")
        rl = const.tile([P, 8], F32, name="rl")
        sp = const.tile([P, 8], F32, name="sp")
        sq = const.tile([P, 8], F32, name="sq")
        nil2c = const.tile([P, 8], F32, name="nil2c")
        nil2 = const.tile([P, D], F32, name="nil2")
        nc.vector.tensor_copy(out=x5[:, 0:T], in_=lsb[:])
        nc.vector.tensor_copy(out=x5[:, T:T + 1], in_=vb[:])
        nc.vector.scalar_tensor_tensor(out=na[:, 0:5], in0=x5[:, 0:5], scalar=-1.0, in1=x5[:, 0:5], op0=ALU.mult, op1=ALU.min)
        nc.vector.tensor_scalar(out=rl[:, 0:5], in0=x5[:, 0:5], scalar1=0.0, scalar2=None, op0=ALU.max)
        nc.scalar.activation(out=na[:, 0:5], in_=na[:, 0:5], func=ACT.Exp)
        nc.scalar.activation(out=na[:, 0:5], in_=na[:, 0:5], func=ACT.Ln, bias=1.0)
        nc.vector.tensor_tensor(out=sp[:, 0:5], in0=na[:, 0:5], in1=rl[:, 0:5], op=ALU.add)
        vcol = sp[:, T:T + 1]

        def params_l():
            nc.vector.tensor_tensor(out=sq[:, 0:T], in0=sp[:, 0:T], in1=sp[:, 0:T], op=ALU.mult)
            nc.vector.reciprocal(out=sq[:, 0:T], in_=sq[:, 0:T])
            nc.vector.tensor_scalar(out=nil2c[:, 0:T], in0=sq[:, 0:T], scalar1=-1.0, scalar2=None, op0=ALU.mult)
            pb = psum.tile([P, D], F32, name="pb", tag="mx", bufs=MXB)
            for c in range(T):
                nc.tensor.matmul(out=pb[:, c * P:(c + 1) * P], lhsT=nil2c[:, c:c + 1].to_broadcast([P, P]), rhs=ident[:],
                                 start=True, stop=True)
            nc.scalar.copy(out=nil2[:].rearrange("p (n c) -> p n c", c=T), in_=pb[:].rearrange("p (c n) -> p n c", c=T))

        etiles = {}
        gmtiles = {}
        wtiles = {}
        trtiles = {}
        smtiles = {}
        abtiles = {}
        bbtiles = {}
        acodes = {}
        bcodes = {}
        free_a = list(range(16))
        free_b = list(range(16))
        slot_a = {}
        slot_b = {}

        def s_exp(n):
            e = stream.tile([P, T, KP], F32, name="e", tag="e", bufs=2)
            etiles[n] = e
            if n == 0:
                for t in range(T):
                    nc.scalar.activation(out=e[:, t, :], in_=dtiles[n][t][:], func=ACT.Exp, scale=-0.5)
                return
            nc.scalar.activation(
                out=e[:].rearrange("p t j -> p (t j)"),
                in_=dtiles[n][:].rearrange("p t j -> p (t j)"),
                func=ACT.Exp, scale=-0.5)
            etiles[n] = e

        def v_mask(n):
            gm = stream.tile([P, T, KP], BF16, name="gm", tag="gm", bufs=2)
            gmtiles[n] = gm
            if n == 0:
                for t in range(T):
                    nc.vector.scalar_tensor_tensor(out=gm[:, t, :], in0=dtiles[n][t][:], scalar=0.0, in1=gtiles[n][t][:],
                                                   op0=ALU.is_gt, op1=ALU.mult)
                return
            nc.vector.scalar_tensor_tensor(
                out=gm[:].rearrange("p t j -> p (t j)"),
                in0=dtiles[n][:].rearrange("p t j -> p (t j)"), scalar=0.0,
                in1=gtiles[n][:].rearrange("p t j -> p (t j)"),
                op0=ALU.is_gt, op1=ALU.mult)
            gmtiles[n] = gm

        def v_product(n):
            gi, gj = seq[n]
            w = stream.tile([P, T, KP], F32, name="w", tag="w", bufs=2)
            for t in range(T):
                col = (gi * T + t) * G + gj
                nc.vector.scalar_tensor_tensor(
                    out=w[:, t, :].rearrange("p (u q) -> p q u", u=T),
                    in0=etiles[n][:, t, :].rearrange("p (q u) -> p q u", u=T),
                    scalar=vcol,
                    in1=gmtiles[n][:, t, :].rearrange("p (q u) -> p q u", u=T),
                    op0=ALU.mult, op1=ALU.mult,
                    accum_out=rpart[:, col:col + 1])
            wtiles[n] = w

        def pe_transposes(n):
            gi, gj = seq[n]
            w = wtiles[n]
            trs = []
            for t in range(T):
                tr = psum.tile([P, T, P], F32, name="tr", tag="tr", bufs=TRB)
                for u in range(T):
                    nc.tensor.transpose(out=tr[:, u, :], in_=w[:, t, u * P:(u + 1) * P], identity=ident[:])
                trs.append(tr)
            sm = psum.tile([P, T, P], F32, name="sm", tag="sm", bufs=SMB)
            for u in range(T):
                for t in range(T):
                    nc.tensor.matmul(out=sm[:, u, :], lhsT=w[:, t, u * P:(u + 1) * P], rhs=ident[:],
                                     start=(t == 0), stop=(t == T - 1), is_transpose=True)
            trtiles[n] = trs
            smtiles[n] = sm

        def v_csum(n):
            gi, gj = seq[n]
            nc.vector.tensor_reduce(out=cpart[:, gj, :, gi], in_=smtiles[n][:], axis=AX.X, op=ALU.add)

        def s_csum(n):
            gi, gj = seq[n]
            junk = stream.tile([P, T, P], BF16, name="junk", tag="junk", bufs=1)
            for u in range(T):
                nc.scalar.activation(out=junk[:, u, :], in_=smtiles[n][:, u, :], func=ACT.Copy,
                                     accum_out=cpart[:, gj, u, gi:gi + 1])

        def s_aint(n):
            ab = stream.tile([P, KP, T], BF16, name="ab", tag="ab", bufs=2, align_bytes=64)
            nc.scalar.copy(out=ab[:].rearrange("p (c i) t -> p c t i", i=4),
                           in_=wtiles[n][:].rearrange("p t (c i) -> p c t i", i=4))
            abtiles[n] = ab

        def s_bout(n):
            bb = stream.tile([P, T, P, T], BF16, name="bb", tag="bb", bufs=2, align_bytes=64)
            for t in range(T):
                nc.scalar.copy(out=bb[:, t], in_=trtiles[n][t][:].rearrange("p u c -> p c u"))
            bbtiles[n] = bb

        def v_quant(n):
            sa = free_a.pop(0)
            sb = free_b.pop(0)
            slot_a[n] = sa
            slot_b[n] = sb
            ac = codes.tile([P, KP], U32, name="ac%d" % sa, tag="ac%d" % sa, align_bytes=64)
            asc = codes.tile([P, KP], U8, name="as%d" % sa, tag="as%d" % sa, align_bytes=64)
            bc = codes.tile([P, KP], U32, name="bc%d" % sb, tag="bc%d" % sb, align_bytes=64)
            bsc = codes.tile([P, KP], U8, name="bs%d" % sb, tag="bs%d" % sb, align_bytes=64)
            nc.vector.quantize_mx(out=ac[:].bitcast(E5), scales=asc[:],
                                  in_=abtiles[n][:].rearrange("p j t -> p (j t)"))
            nc.vector.quantize_mx(out=bc[:].bitcast(E5), scales=bsc[:],
                                  in_=bbtiles[n][:].rearrange("p t c u -> p (t c u)"))
            acodes[seq[n]] = (ac, asc)
            bcodes[seq[n]] = (bc, bsc)

        xstage = {}

        def v_xcopy(which, g):
            st = stream.tile([P, D, T], BF16, name="xst", tag="xst", bufs=2, align_bytes=64)
            src = x2n if which == 2 else xn
            if (which, g) in XINT_S:
                nc.scalar.copy(out=st[:].rearrange("p (c i) t -> p c t i", i=4),
                               in_=src[g][:].rearrange("p t (c i) -> p c t i", i=4))
            else:
                nc.vector.tensor_copy(out=st[:].rearrange("p (c i) t -> p c t i", i=4),
                                      in_=src[g][:].rearrange("p t (c i) -> p c t i", i=4))
            xstage[(which, g)] = st

        def v_xquant(which, g):
            c_, s_ = (x2c, x2s) if which == 2 else (xc, xs)
            nc.vector.quantize_mx(out=c_[:, g, :].bitcast(E4), scales=s_[:, g, :],
                                  in_=xstage[(which, g)][:].rearrange("p k t -> p (k t)"))

        def pe_job(job):
            kind, g, t = job
            acc = psum.tile([P, D], F32, name="acc", tag="mx", bufs=MXB)
            for h in range(G):
                if kind == 0:
                    lc, ls = bcodes[(g, h)]
                    rc, rsc = x2c, x2s
                else:
                    lc, ls = acodes[(h, g)]
                    rc, rsc = xc, xs
                nc.tensor.matmul_mx(
                    out=acc[:],
                    lhsT=lc[:, t * P:(t + 1) * P].bitcast(E5), lhsT_scale=ls[:, t * P:(t + 1) * P],
                    rhs=rc[:, h, :].bitcast(E4), rhs_scale=rsc[:, h, :],
                    start=(h == 0), stop=(h == G - 1))
            return acc

        def v_epi1(job, acc):
            kind, g, t = job
            src, sums = (xn, rs) if kind == 0 else (x2n, cs)
            z = stream.tile([P, D], F32, name="z", tag="z", bufs=4)
            nc.vector.scalar_tensor_tensor(out=z[:], in0=src[g][:, t, :], scalar=sums[:, g * T + t:g * T + t + 1],
                                           in1=acc[:], op0=ALU.mult, op1=ALU.subtract)
            return z

        def v_epi2(job, z):
            kind, g, t = job
            dst = o0v if kind == 0 else o1v
            o = stream.tile([P, D], F32, name="o", tag="o", bufs=4)
            nc.vector.tensor_tensor(out=o[:], in0=z[:], in1=nil2[:], op=ALU.mult)
            nc.sync.dma_start(out=dst[:, g, t, :], in_=o[:])

        done_rows = [0] * G
        done_cols = [0] * G

        for s in range(nb + 2):
            if s + 2 < nb:
                load(s + 2)
            if s < 4:
                load_x(1, s)
            if s < nb:
                s_exp(s)
            jobs = []
            if s >= 2:
                n = s - 2
                v_quant(n)
                if not CSUM_S:
                    v_csum(n)
                gi, gj = seq[n]
                done_rows[gi] += 1
                done_cols[gj] += 1
                if done_rows[gi] == G:
                    jobs.extend([(0, gi, t) for t in range(T)])
                if done_cols[gj] == G:
                    jobs.extend([(1, gj, t) for t in range(T)])
            if 1 <= s <= 8:
                v_xquant(2 if s <= 4 else 1, (s - 1) % 4)
            if s == 0:
                v_mask(0)
            if s + 1 < nb:
                v_mask(s + 1)
            if 1 <= s <= nb:
                pe_transposes(s - 1)
                s_aint(s - 1)
                s_bout(s - 1)
                if CSUM_S:
                    s_csum(s - 1)
            if s < nb:
                v_product(s)
            if s == 0:
                params_l()
            if s < 8:
                v_xcopy(2 if s < 4 else 1, s % 4)
            for job in jobs:
                kind, g, t = job
                if t == 0:
                    if kind == 0:
                        nc.vector.tensor_reduce(out=rs[:, g * T:(g + 1) * T],
                                                in_=rpart[:, g * T * G:(g + 1) * T * G].rearrange("p (t n) -> p t n", n=G),
                                                axis=AX.X, op=ALU.add)
                    else:
                        nc.vector.tensor_reduce(out=cs[:, g * T:(g + 1) * T],
                                                in_=cpart[:, g],
                                                axis=AX.X, op=ALU.add)
            for i in range(0, len(jobs), 2):
                acc_a = pe_job(jobs[i])
                acc_b = pe_job(jobs[i + 1])
                z_a = v_epi1(jobs[i], acc_a)
                z_b = v_epi1(jobs[i + 1], acc_b)
                v_epi2(jobs[i], z_a)
                v_epi2(jobs[i + 1], z_b)
            for job in jobs:
                kind, g, t = job
                if t == T - 1:
                    for n in range(nb):
                        if kind == 0 and seq[n][0] == g:
                            free_b.append(slot_b[n])
                            free_b.sort()
                        if kind == 1 and seq[n][1] == g:
                            free_a.append(slot_a[n])
                            free_a.sort()
